import numpy as np
import ml_dtypes


def mxq(x, axis, fmt="e4m3"):
    dtype, down = {"e4m3": (ml_dtypes.float8_e4m3fn, 7), "e5m2": (ml_dtypes.float8_e5m2, 14)}[fmt]
    v = np.moveaxis(np.asarray(x, np.float32).astype(ml_dtypes.bfloat16).astype(np.float64), axis, -1)
    blocks = v.reshape(v.shape[:-1] + (-1, 32))
    amax = np.abs(blocks).max(-1, keepdims=True)
    byte = np.maximum(np.where(amax > 0, np.frexp(amax)[1] - 1 + 127, 0) - down, 1)
    scale = np.exp2(byte - 127.0)
    codes = (blocks / scale).astype(np.float32).astype(dtype).astype(np.float64)
    return np.moveaxis((codes * scale).reshape(v.shape), -1, axis)


WIDE = False


def mx_kscale(k):
    if not WIDE:
        return np.ones(k)
    levels = np.array([10, -10, 5, -5, 0])
    if k % 512:
        return np.exp2(np.random.permutation(np.resize(levels, k // 32))).repeat(32)
    a = np.empty((k // 512, 16))
    for p in range(k // 512):
        a[p, :8] = np.random.permutation(np.resize(levels, 8))
        for g in range(8):
            far = levels[np.abs(levels - a[p, g]) >= 10]
            a[p, g + 8] = far[np.random.randint(len(far))]
    return np.exp2(a.ravel()).repeat(32)


BF16 = ml_dtypes.bfloat16


def bf(x):
    return np.asarray(x, np.float32).astype(BF16)


def f64(x):
    return np.asarray(x).astype(np.float64)


E2M1 = np.array([0.0, 0.5, 1.0, 1.5, 2.0, 3.0, 4.0, 6.0, -0.0, -0.5, -1.0, -1.5, -2.0, -3.0, -4.0, -6.0])


def pack_weight(w, fmt):
    k, n = w.shape
    w = f64(bf(w)).reshape(k // 32, 32, n)
    amax = np.abs(w).max(1)
    if fmt == "e4m3":
        byte = np.frexp(amax)[1] - 1 + 127 - 7
    else:
        mant, ex = np.frexp(amax / 6.0)
        byte = np.where(mant > 0.5, ex, ex - 1) + 127
    byte = np.clip(np.where(amax > 0, byte, 1), 1, 254)
    scaled = (w * np.exp2(127.0 - byte)[:, None, :]).reshape(k, n).astype(np.float32)
    by_word = np.ascontiguousarray(scaled.reshape(k // 512, 128, 4, n).transpose(0, 1, 3, 2))
    if fmt == "e4m3":
        words = by_word.astype(ml_dtypes.float8_e4m3fn).view(np.uint8)
    else:
        c = by_word.astype(ml_dtypes.float4_e2m1fn).view(np.uint8) & 0xF
        words = c[..., 0::2] | (c[..., 1::2] << 4)
    return np.ascontiguousarray(words), np.ascontiguousarray(byte.astype(np.uint8).reshape(k // 512, 16, n))


def unpack_weight(words, scales, fmt):
    g, p, n, _ = words.shape
    if fmt == "e4m3":
        vals = np.ascontiguousarray(words).view(ml_dtypes.float8_e4m3fn).astype(np.float64)
    else:
        nib = np.empty((g, p, n, 4), np.uint8)
        nib[..., 0::2] = words & 0xF
        nib[..., 1::2] = words >> 4
        vals = E2M1[nib]
    vals = vals * np.repeat(np.exp2(scales.astype(np.float64) - 127.0), 8, axis=1)[..., None]
    return vals.transpose(0, 1, 3, 2).reshape(g * 512, n)


N, NFEAT, NHID, NOUT, NCLS = 1024, 512, 512, 512, 128
SPAN = 60.0
LAM = SPAN * np.log(2.0)
AGG = np.sqrt(LAM / (2.0 * N))


def setup_inputs():
    s, r = mx_kscale(NFEAT), mx_kscale(N)
    x = bf(np.random.standard_normal((N, NFEAT)) * s / r[:, None])
    adj = bf(np.exp2(-SPAN * np.random.uniform(size=(N, N))) * (LAM / N) * r)
    W1_words, W1_scales = pack_weight(np.random.standard_normal((NFEAT, NHID)) * (0.7 / (AGG * np.sqrt(NFEAT))) / s[:, None], "e4m3")
    b1 = bf(np.random.standard_normal(NHID) * 0.3)
    return {
        "x": x,
        "adj": adj,
        "W1_words": W1_words,
        "W1_scales": W1_scales,
        "b1": b1,
    }


def reference(x, adj, W1_words, W1_scales, b1):
    support = mxq(f64(x), 1, "e4m3") @ unpack_weight(W1_words, W1_scales, "e4m3")
    return np.maximum((mxq(f64(adj), 1, "e4m3") @ mxq(support, 0, "e4m3")) + f64(b1), 0.0)

@@ -1,0 +1,158 @@
+from contextlib import ExitStack
+
+import concourse.mybir as mybir
+from concourse.masks import make_identity
+
+F32 = mybir.dt.float32
+BF16 = mybir.dt.bfloat16
+I32 = mybir.dt.int32
+U32 = mybir.dt.uint32
+U8 = mybir.dt.uint8
+FP8X4 = mybir.dt.float8_e4m3fn_x4
+
+P = 128
+PACK = 4
+NODES = 1024
+FEATS = 512
+HIDDEN = 512
+SLOTS = NODES // P
+PASSES = NODES // (P * PACK)
+ROW_TILES = NODES // P
+AHEAD = 3
+
+FLOPS = 2 * NODES * FEATS * HIDDEN + 2 * NODES * NODES * HIDDEN
+
+
+def tile_gcn_pa_kernel(tc, x, adj, W1_words, W1_scales, b1, out):
+    nc = tc.nc
+    with ExitStack() as ctx:
+        ctx.enter_context(tc.manual_schedule())
+        keep = ctx.enter_context(tc.tile_pool(name="keep", bufs=1))
+        banks = ctx.enter_context(tc.psum_pool(name="banks", bufs=8))
+
+        identity = keep.tile([P, P], F32)
+        make_identity(nc, identity[:])
+        w_scales = keep.tile([P, HIDDEN], U8, align_bytes=64)
+        nc.vector.memset(w_scales[:].bitcast(I32), 0)
+        bias_rows = keep.tile([P, HIDDEN], BF16)
+        nc.vector.memset(bias_rows[:], 0.0)
+        ones = keep.tile([P, P], BF16)
+        nc.vector.memset(ones[:], 1.0)
+
+        x_sb = keep.tile([P, SLOTS, FEATS], BF16)
+        x_chunks = x.rearrange("(g p h e) k -> g h p e k", p=P, h=2, e=2)
+
+        def load_x(c):
+            nc.sync.dma_start(out=x_sb[:, 2 * c : 2 * c + 2, :], in_=x_chunks[c // 2, c % 2])
+
+        for c in range(4):
+            load_x(c)
+        nc.sync.dma_start(out=bias_rows[0:1, :], in_=b1.unsqueeze(0))
+        w_codes = keep.tile([P, HIDDEN], U32, align_bytes=64)
+        nc.sync.dma_start(
+            out=w_codes[:].bitcast(I32), in_=W1_words[0].rearrange("p n t -> p (n t)").bitcast(I32)
+        )
+        for quadrant in range(4):
+            nc.sync.dma_start(
+                out=w_scales[32 * quadrant : 32 * quadrant + 4, :].bitcast(I32),
+                in_=W1_scales[0, 4 * quadrant : 4 * quadrant + 4, :].bitcast(I32),
+            )
+
+        adj_sb = keep.tile([P, ROW_TILES, NODES], BF16)
+        adj_rows = adj.rearrange("(p a) j -> p a j", a=ROW_TILES)
+        for a in range(0, ROW_TILES, 2):
+            nc.sync.dma_start(out=adj_sb[:, a : a + 2, :], in_=adj_rows[:, a : a + 2, :])
+
+        x_words = x_sb[:].bitcast(F32)
+
+        x_grouped = keep.tile([P, SLOTS, P, PACK], BF16, align_bytes=64)
+        x_grouped_words = x_grouped[:].bitcast(F32)
+        x_codes = keep.tile([P, SLOTS, P], U32, align_bytes=64)
+        x_scales = keep.tile([P, SLOTS, P], U8, align_bytes=64)
+        for c in range(4):
+            slots = slice(2 * c, 2 * c + 2)
+            xt = banks.tile([P, 2, 2, P], F32, tag="bank")
+            for e in range(2):
+                for v in range(2):
+                    nc.tensor.transpose(xt[:, e, v, :], x_words[:, 2 * c + e, v : FEATS // 2 : 2], identity[:])
+            nc.scalar.copy(out=x_grouped_words[:, slots], in_=xt[:].rearrange("p e v j -> p e j v"))
+            nc.vector.quantize_mx(
+                out=x_codes[:, slots, :].rearrange("p s j -> p (s j)").bitcast(FP8X4),
+                scales=x_scales[:, slots, :].rearrange("p s j -> p (s j)"),
+                in_=x_grouped[:, slots].rearrange("p s j t -> p (s j t)"),
+            )
+
+        bias_bank = banks.tile([P, HIDDEN], F32, tag="bank")
+        nc.tensor.matmul(out=bias_bank[:], lhsT=ones[:], rhs=bias_rows[:], start=True, stop=True)
+        bias = keep.tile([P, HIDDEN], F32)
+        nc.scalar.copy(out=bias[:], in_=bias_bank[:])
+
+        s_grouped = keep.tile([P, PASSES, HIDDEN, PACK], BF16, align_bytes=64)
+        s_codes = keep.tile([P, PASSES, HIDDEN], U32, align_bytes=64)
+        s_scales = keep.tile([P, PASSES, HIDDEN], U8, align_bytes=64)
+        for g in range(PASSES):
+            for c in range(HIDDEN // P):
+                cols = slice(P * c, P * (c + 1))
+                sup = banks.tile([P, PACK, P], F32, tag="bank")
+                for t in range(PACK):
+                    nc.tensor.matmul_mx(
+                        out=sup[:, t, :],
+                        lhsT=x_codes[:, PACK * g + t, :].bitcast(FP8X4),
+                        lhsT_scale=x_scales[:, PACK * g + t, :],
+                        rhs=w_codes[:, cols].bitcast(FP8X4),
+                        rhs_scale=w_scales[:, cols],
+                        start=True,
+                        stop=True,
+                    )
+                copy = nc.vector.tensor_copy if c % 2 == 0 else nc.scalar.copy
+                copy(out=s_grouped[:, g, cols, :], in_=sup[:].rearrange("p t n -> p n t"))
+            nc.vector.quantize_mx(
+                out=s_codes[:, g, :].bitcast(FP8X4),
+                scales=s_scales[:, g, :],
+                in_=s_grouped[:, g].rearrange("p n t -> p (n t)"),
+            )
+
+        adj_words = adj_sb[:].bitcast(F32)
+        a_grouped = keep.tile([P, ROW_TILES, PASSES, P, PACK], BF16, align_bytes=64)
+        a_grouped_words = a_grouped[:].bitcast(F32)
+        a_codes = keep.tile([P, ROW_TILES, PASSES, P], U32, align_bytes=64)
+        a_scales = keep.tile([P, ROW_TILES, PASSES, P], U8, align_bytes=64)
+        for a in range(ROW_TILES):
+            at = banks.tile([P, PASSES, 2, P], F32, tag="bank")
+            for g in range(PASSES):
+                for u in range(2):
+                    words = slice(2 * P * g + u, 2 * P * (g + 1), 2)
+                    nc.tensor.transpose(at[:, g, u, :], adj_words[:, a, words], identity[:])
+            nc.scalar.copy(out=a_grouped_words[:, a], in_=at[:].rearrange("p g u i -> p g i u"))
+
+        def quantise_adj(a):
+            nc.vector.quantize_mx(
+                out=a_codes[:, a].rearrange("p g i -> p (g i)").bitcast(FP8X4),
+                scales=a_scales[:, a].rearrange("p g i -> p (g i)"),
+                in_=a_grouped[:, a].rearrange("p g i t -> p (g i t)"),
+            )
+
+        summed = keep.tile([P, ROW_TILES, HIDDEN], F32)
+        result = keep.tile([P, ROW_TILES, HIDDEN], F32)
+        out_rows = out.rearrange("(p a) n -> p a n", a=ROW_TILES)
+        for a in range(AHEAD):
+            quantise_adj(a)
+        for a in range(ROW_TILES):
+            if a + AHEAD < ROW_TILES:
+                quantise_adj(a + AHEAD)
+            acc = banks.tile([P, HIDDEN], F32, tag="bank")
+            for g in range(PASSES):
+                nc.tensor.matmul_mx(
+                    out=acc[:],
+                    lhsT=a_codes[:, a, g, :].bitcast(FP8X4),
+                    lhsT_scale=a_scales[:, a, g, :],
+                    rhs=s_codes[:, g, :].bitcast(FP8X4),
+                    rhs_scale=s_scales[:, g, :],
+                    start=(g == 0),
+                    stop=(g == PASSES - 1),
+                )
+            nc.vector.tensor_tensor(out=summed[:, a, :], in0=acc[:], in1=bias[:], op=mybir.AluOpType.add)
+            nc.scalar.activation(
+                out=result[:, a, :], in_=summed[:, a, :], func=mybir.ActivationFunctionType.Relu
+            )
+            nc.sync.dma_start(out=out_rows[:, a, :], in_=result[:, a, :])

@@ -9,6 +9,8 @@ I32 = mybir.dt.int32
 U32 = mybir.dt.uint32
 U8 = mybir.dt.uint8
 FP8X4 = mybir.dt.float8_e4m3fn_x4
+RELU = mybir.ActivationFunctionType.Relu
+ALU = mybir.AluOpType
 
 P = 128
 PACK = 4
@@ -18,7 +20,8 @@ HIDDEN = 512
 SLOTS = NODES // P
 PASSES = NODES // (P * PACK)
 ROW_TILES = NODES // P
-AHEAD = 3
+CHUNKS = 4
+WARM_UP = 16
 
 FLOPS = 2 * NODES * FEATS * HIDDEN + 2 * NODES * NODES * HIDDEN
 
@@ -30,46 +33,44 @@ def tile_gcn_pa_kernel(tc, x, adj, W1_words, W1_scales, b1, out):
         keep = ctx.enter_context(tc.tile_pool(name="keep", bufs=1))
         banks = ctx.enter_context(tc.psum_pool(name="banks", bufs=8))
 
-        identity = keep.tile([P, P], F32)
-        make_identity(nc, identity[:])
-        w_scales = keep.tile([P, HIDDEN], U8, align_bytes=64)
-        nc.vector.memset(w_scales[:].bitcast(I32), 0)
-        bias_rows = keep.tile([P, HIDDEN], BF16)
-        nc.vector.memset(bias_rows[:], 0.0)
         ones = keep.tile([P, P], BF16)
         nc.vector.memset(ones[:], 1.0)
+        bias_rows = keep.tile([P, HIDDEN], BF16)
+        nc.vector.memset(bias_rows[:].bitcast(I32), 0)
+        nc.scalar.dma_start(out=bias_rows[0:1, :], in_=b1.unsqueeze(0))
+        identity = keep.tile([P, P], F32)
+        make_identity(nc, identity[:])
 
         x_sb = keep.tile([P, SLOTS, FEATS], BF16)
         x_chunks = x.rearrange("(g p h e) k -> g h p e k", p=P, h=2, e=2)
-
-        def load_x(c):
+        for c in range(CHUNKS):
             nc.sync.dma_start(out=x_sb[:, 2 * c : 2 * c + 2, :], in_=x_chunks[c // 2, c % 2])
-
-        for c in range(4):
-            load_x(c)
-        nc.sync.dma_start(out=bias_rows[0:1, :], in_=b1.unsqueeze(0))
         w_codes = keep.tile([P, HIDDEN], U32, align_bytes=64)
         nc.sync.dma_start(
             out=w_codes[:].bitcast(I32), in_=W1_words[0].rearrange("p n t -> p (n t)").bitcast(I32)
         )
+        w_scales = keep.tile([P, HIDDEN], U8, align_bytes=64)
         for quadrant in range(4):
+            rows = W1_scales[0, 4 * quadrant : 4 * quadrant + 4, :].bitcast(I32)
             nc.sync.dma_start(
-                out=w_scales[32 * quadrant : 32 * quadrant + 4, :].bitcast(I32),
-                in_=W1_scales[0, 4 * quadrant : 4 * quadrant + 4, :].bitcast(I32),
+                out=w_scales[32 * quadrant : 32 * quadrant + 32, :].bitcast(I32),
+                in_=rows.unsqueeze(0).to_broadcast([8, 4, HIDDEN // 4]),
             )
-
         adj_sb = keep.tile([P, ROW_TILES, NODES], BF16)
         adj_rows = adj.rearrange("(p a) j -> p a j", a=ROW_TILES)
         for a in range(0, ROW_TILES, 2):
             nc.sync.dma_start(out=adj_sb[:, a : a + 2, :], in_=adj_rows[:, a : a + 2, :])
 
-        x_words = x_sb[:].bitcast(F32)
+        idle_bank = banks.tile([P, P], F32, tag="bank")
+        for i in range(WARM_UP):
+            nc.tensor.matmul(out=idle_bank[:], lhsT=ones[:], rhs=ones[:], start=True, stop=True)
 
+        x_words = x_sb[:].bitcast(F32)
         x_grouped = keep.tile([P, SLOTS, P, PACK], BF16, align_bytes=64)
         x_grouped_words = x_grouped[:].bitcast(F32)
         x_codes = keep.tile([P, SLOTS, P], U32, align_bytes=64)
         x_scales = keep.tile([P, SLOTS, P], U8, align_bytes=64)
-        for c in range(4):
+        for c in range(CHUNKS):
             slots = slice(2 * c, 2 * c + 2)
             xt = banks.tile([P, 2, 2, P], F32, tag="bank")
             for e in range(2):
@@ -82,14 +83,19 @@ def tile_gcn_pa_kernel(tc, x, adj, W1_words, W1_scales, b1, out):
                 in_=x_grouped[:, slots].rearrange("p s j t -> p (s j t)"),
             )
 
-        bias_bank = banks.tile([P, HIDDEN], F32, tag="bank")
-        nc.tensor.matmul(out=bias_bank[:], lhsT=ones[:], rhs=bias_rows[:], start=True, stop=True)
-        bias = keep.tile([P, HIDDEN], F32)
-        nc.scalar.copy(out=bias[:], in_=bias_bank[:])
-
         s_grouped = keep.tile([P, PASSES, HIDDEN, PACK], BF16, align_bytes=64)
         s_codes = keep.tile([P, PASSES, HIDDEN], U32, align_bytes=64)
         s_scales = keep.tile([P, PASSES, HIDDEN], U8, align_bytes=64)
+
+        bias = keep.tile([P, HIDDEN], F32)
+
+        def quantise_support(g, cols):
+            nc.vector.quantize_mx(
+                out=s_codes[:, g, cols].bitcast(FP8X4),
+                scales=s_scales[:, g, cols],
+                in_=s_grouped[:, g, cols].rearrange("p n t -> p (n t)"),
+            )
+
         for g in range(PASSES):
             for c in range(HIDDEN // P):
                 cols = slice(P * c, P * (c + 1))
@@ -104,26 +110,34 @@ def tile_gcn_pa_kernel(tc, x, adj, W1_words, W1_scales, b1, out):
                         start=True,
                         stop=True,
                     )
-                copy = nc.vector.tensor_copy if c % 2 == 0 else nc.scalar.copy
+                if g == 1 and c == 1:
+                    quantise_support(0, slice(0, HIDDEN))
+                copy = nc.vector.tensor_copy if (g, c) in ((0, 1), (0, 3), (1, 1)) else nc.scalar.copy
                 copy(out=s_grouped[:, g, cols, :], in_=sup[:].rearrange("p t n -> p n t"))
-            nc.vector.quantize_mx(
-                out=s_codes[:, g, :].bitcast(FP8X4),
-                scales=s_scales[:, g, :],
-                in_=s_grouped[:, g].rearrange("p n t -> p (n t)"),
-            )
+            if g == 0:
+                bias_bank = banks.tile([P, HIDDEN], F32, tag="bank")
+                nc.tensor.matmul(out=bias_bank[:], lhsT=ones[:], rhs=bias_rows[:], start=True, stop=True)
+                nc.vector.tensor_copy(out=bias[:], in_=bias_bank[:])
+        for half in range(2):
+            quantise_support(1, slice(HIDDEN // 2 * half, HIDDEN // 2 * (half + 1)))
 
         adj_words = adj_sb[:].bitcast(F32)
         a_grouped = keep.tile([P, ROW_TILES, PASSES, P, PACK], BF16, align_bytes=64)
         a_grouped_words = a_grouped[:].bitcast(F32)
         a_codes = keep.tile([P, ROW_TILES, PASSES, P], U32, align_bytes=64)
         a_scales = keep.tile([P, ROW_TILES, PASSES, P], U8, align_bytes=64)
-        for a in range(ROW_TILES):
+        turned = {}
+
+        def transpose_adj(a):
             at = banks.tile([P, PASSES, 2, P], F32, tag="bank")
             for g in range(PASSES):
-                for u in range(2):
-                    words = slice(2 * P * g + u, 2 * P * (g + 1), 2)
-                    nc.tensor.transpose(at[:, g, u, :], adj_words[:, a, words], identity[:])
-            nc.scalar.copy(out=a_grouped_words[:, a], in_=at[:].rearrange("p g u i -> p g i u"))
+                for v in range(2):
+                    words = slice(2 * P * g + v, 2 * P * (g + 1), 2)
+                    nc.tensor.transpose(at[:, g, v, :], adj_words[:, a, words], identity[:])
+            turned[a] = at
+
+        def group_adj(a):
+            nc.scalar.copy(out=a_grouped_words[:, a], in_=turned[a][:].rearrange("p g v i -> p g i v"))
 
         def quantise_adj(a):
             nc.vector.quantize_mx(
@@ -135,11 +149,9 @@ def tile_gcn_pa_kernel(tc, x, adj, W1_words, W1_scales, b1, out):
         summed = keep.tile([P, ROW_TILES, HIDDEN], F32)
         result = keep.tile([P, ROW_TILES, HIDDEN], F32)
         out_rows = out.rearrange("(p a) n -> p a n", a=ROW_TILES)
-        for a in range(AHEAD):
-            quantise_adj(a)
-        for a in range(ROW_TILES):
-            if a + AHEAD < ROW_TILES:
-                quantise_adj(a + AHEAD)
+        sums = {}
+
+        def multiply(a):
             acc = banks.tile([P, HIDDEN], F32, tag="bank")
             for g in range(PASSES):
                 nc.tensor.matmul_mx(
@@ -151,8 +163,33 @@ def tile_gcn_pa_kernel(tc, x, adj, W1_words, W1_scales, b1, out):
                     start=(g == 0),
                     stop=(g == PASSES - 1),
                 )
-            nc.vector.tensor_tensor(out=summed[:, a, :], in0=acc[:], in1=bias[:], op=mybir.AluOpType.add)
-            nc.scalar.activation(
-                out=result[:, a, :], in_=summed[:, a, :], func=mybir.ActivationFunctionType.Relu
+            sums[a] = acc
+
+        def finish(a, cols):
+            nc.vector.tensor_tensor(
+                out=summed[:, a, cols], in0=sums[a][:, cols], in1=bias[:, cols], op=ALU.add
             )
-            nc.sync.dma_start(out=out_rows[:, a, :], in_=result[:, a, :])
+            nc.scalar.activation(out=result[:, a, cols], in_=summed[:, a, cols], func=RELU)
+            nc.sync.dma_start(out=out_rows[:, a, cols], in_=result[:, a, cols])
+
+        for a in range(5):
+            transpose_adj(a)
+        for a in range(4):
+            group_adj(a)
+        for a in range(3):
+            quantise_adj(a)
+        for pair in range(0, ROW_TILES, 2):
+            for a in (pair, pair + 1):
+                multiply(a)
+            for a in (pair + 5, pair + 6):
+                if a < ROW_TILES:
+                    transpose_adj(a)
+            for a in (pair, pair + 1):
+                if a + 4 < ROW_TILES:
+                    group_adj(a + 4)
+                halves = 2 if a == ROW_TILES - 1 else 1
+                width = HIDDEN // halves
+                for h in range(halves):
+                    finish(a, slice(width * h, width * (h + 1)))
+                if a + 3 < ROW_TILES:
+                    quantise_adj(a + 3)

from contextlib import ExitStack

import concourse.mybir as mybir
from concourse.masks import make_identity

F32 = mybir.dt.float32
BF16 = mybir.dt.bfloat16
I32 = mybir.dt.int32
U32 = mybir.dt.uint32
U8 = mybir.dt.uint8
FP8X4 = mybir.dt.float8_e4m3fn_x4
RELU = mybir.ActivationFunctionType.Relu
ALU = mybir.AluOpType

P = 128
PACK = 4
NODES = 1024
FEATS = 512
HIDDEN = 512
SLOTS = NODES // P
PASSES = NODES // (P * PACK)
ROW_TILES = NODES // P
CHUNKS = 4
WARM_UP = 16

FLOPS = 2 * NODES * FEATS * HIDDEN + 2 * NODES * NODES * HIDDEN


def tile_gcn_pa_kernel(tc, x, adj, W1_words, W1_scales, b1, out):
    nc = tc.nc
    with ExitStack() as ctx:
        ctx.enter_context(tc.manual_schedule())
        keep = ctx.enter_context(tc.tile_pool(name="keep", bufs=1))
        banks = ctx.enter_context(tc.psum_pool(name="banks", bufs=8))

        ones = keep.tile([P, P], BF16)
        nc.vector.memset(ones[:], 1.0)
        bias_rows = keep.tile([P, HIDDEN], BF16)
        nc.vector.memset(bias_rows[:].bitcast(I32), 0)
        nc.scalar.dma_start(out=bias_rows[0:1, :], in_=b1.unsqueeze(0))
        identity = keep.tile([P, P], F32)
        make_identity(nc, identity[:])

        x_sb = keep.tile([P, SLOTS, FEATS], BF16)
        x_chunks = x.rearrange("(g p h e) k -> g h p e k", p=P, h=2, e=2)
        for c in range(CHUNKS):
            nc.sync.dma_start(out=x_sb[:, 2 * c : 2 * c + 2, :], in_=x_chunks[c // 2, c % 2])
        w_codes = keep.tile([P, HIDDEN], U32, align_bytes=64)
        nc.sync.dma_start(
            out=w_codes[:].bitcast(I32), in_=W1_words[0].rearrange("p n t -> p (n t)").bitcast(I32)
        )
        w_scales = keep.tile([P, HIDDEN], U8, align_bytes=64)
        for quadrant in range(4):
            rows = W1_scales[0, 4 * quadrant : 4 * quadrant + 4, :].bitcast(I32)
            nc.sync.dma_start(
                out=w_scales[32 * quadrant : 32 * quadrant + 32, :].bitcast(I32),
                in_=rows.unsqueeze(0).to_broadcast([8, 4, HIDDEN // 4]),
            )
        adj_sb = keep.tile([P, ROW_TILES, NODES], BF16)
        adj_rows = adj.rearrange("(p a) j -> p a j", a=ROW_TILES)
        for a in range(0, ROW_TILES, 2):
            nc.sync.dma_start(out=adj_sb[:, a : a + 2, :], in_=adj_rows[:, a : a + 2, :])

        idle_bank = banks.tile([P, P], F32, tag="bank")
        for i in range(WARM_UP):
            nc.tensor.matmul(out=idle_bank[:], lhsT=ones[:], rhs=ones[:], start=True, stop=True)

        x_words = x_sb[:].bitcast(F32)
        x_grouped = keep.tile([P, SLOTS, P, PACK], BF16, align_bytes=64)
        x_grouped_words = x_grouped[:].bitcast(F32)
        x_codes = keep.tile([P, SLOTS, P], U32, align_bytes=64)
        x_scales = keep.tile([P, SLOTS, P], U8, align_bytes=64)
        for c in range(CHUNKS):
            slots = slice(2 * c, 2 * c + 2)
            xt = banks.tile([P, 2, 2, P], F32, tag="bank")
            for e in range(2):
                for v in range(2):
                    nc.tensor.transpose(xt[:, e, v, :], x_words[:, 2 * c + e, v : FEATS // 2 : 2], identity[:])
            nc.scalar.copy(out=x_grouped_words[:, slots], in_=xt[:].rearrange("p e v j -> p e j v"))
            nc.vector.quantize_mx(
                out=x_codes[:, slots, :].rearrange("p s j -> p (s j)").bitcast(FP8X4),
                scales=x_scales[:, slots, :].rearrange("p s j -> p (s j)"),
                in_=x_grouped[:, slots].rearrange("p s j t -> p (s j t)"),
            )

        s_grouped = keep.tile([P, PASSES, HIDDEN, PACK], BF16, align_bytes=64)
        s_codes = keep.tile([P, PASSES, HIDDEN], U32, align_bytes=64)
        s_scales = keep.tile([P, PASSES, HIDDEN], U8, align_bytes=64)

        bias = keep.tile([P, HIDDEN], F32)

        def quantise_support(g, cols):
            nc.vector.quantize_mx(
                out=s_codes[:, g, cols].bitcast(FP8X4),
                scales=s_scales[:, g, cols],
                in_=s_grouped[:, g, cols].rearrange("p n t -> p (n t)"),
            )

        for g in range(PASSES):
            for c in range(HIDDEN // P):
                cols = slice(P * c, P * (c + 1))
                sup = banks.tile([P, PACK, P], F32, tag="bank")
                for t in range(PACK):
                    nc.tensor.matmul_mx(
                        out=sup[:, t, :],
                        lhsT=x_codes[:, PACK * g + t, :].bitcast(FP8X4),
                        lhsT_scale=x_scales[:, PACK * g + t, :],
                        rhs=w_codes[:, cols].bitcast(FP8X4),
                        rhs_scale=w_scales[:, cols],
                        start=True,
                        stop=True,
                    )
                if g == 1 and c == 1:
                    quantise_support(0, slice(0, HIDDEN))
                copy = nc.vector.tensor_copy if (g, c) in ((0, 1), (0, 3), (1, 1)) else nc.scalar.copy
                copy(out=s_grouped[:, g, cols, :], in_=sup[:].rearrange("p t n -> p n t"))
            if g == 0:
                bias_bank = banks.tile([P, HIDDEN], F32, tag="bank")
                nc.tensor.matmul(out=bias_bank[:], lhsT=ones[:], rhs=bias_rows[:], start=True, stop=True)
                nc.vector.tensor_copy(out=bias[:], in_=bias_bank[:])
        for half in range(2):
            quantise_support(1, slice(HIDDEN // 2 * half, HIDDEN // 2 * (half + 1)))

        adj_words = adj_sb[:].bitcast(F32)
        a_grouped = keep.tile([P, ROW_TILES, PASSES, P, PACK], BF16, align_bytes=64)
        a_grouped_words = a_grouped[:].bitcast(F32)
        a_codes = keep.tile([P, ROW_TILES, PASSES, P], U32, align_bytes=64)
        a_scales = keep.tile([P, ROW_TILES, PASSES, P], U8, align_bytes=64)
        turned = {}

        def transpose_adj(a):
            at = banks.tile([P, PASSES, 2, P], F32, tag="bank")
            for g in range(PASSES):
                for v in range(2):
                    words = slice(2 * P * g + v, 2 * P * (g + 1), 2)
                    nc.tensor.transpose(at[:, g, v, :], adj_words[:, a, words], identity[:])
            turned[a] = at

        def group_adj(a):
            nc.scalar.copy(out=a_grouped_words[:, a], in_=turned[a][:].rearrange("p g v i -> p g i v"))

        def quantise_adj(a):
            nc.vector.quantize_mx(
                out=a_codes[:, a].rearrange("p g i -> p (g i)").bitcast(FP8X4),
                scales=a_scales[:, a].rearrange("p g i -> p (g i)"),
                in_=a_grouped[:, a].rearrange("p g i t -> p (g i t)"),
            )

        summed = keep.tile([P, ROW_TILES, HIDDEN], F32)
        result = keep.tile([P, ROW_TILES, HIDDEN], F32)
        out_rows = out.rearrange("(p a) n -> p a n", a=ROW_TILES)
        sums = {}

        def multiply(a):
            acc = banks.tile([P, HIDDEN], F32, tag="bank")
            for g in range(PASSES):
                nc.tensor.matmul_mx(
                    out=acc[:],
                    lhsT=a_codes[:, a, g, :].bitcast(FP8X4),
                    lhsT_scale=a_scales[:, a, g, :],
                    rhs=s_codes[:, g, :].bitcast(FP8X4),
                    rhs_scale=s_scales[:, g, :],
                    start=(g == 0),
                    stop=(g == PASSES - 1),
                )
            sums[a] = acc

        def finish(a, cols):
            nc.vector.tensor_tensor(
                out=summed[:, a, cols], in0=sums[a][:, cols], in1=bias[:, cols], op=ALU.add
            )
            nc.scalar.activation(out=result[:, a, cols], in_=summed[:, a, cols], func=RELU)
            nc.sync.dma_start(out=out_rows[:, a, cols], in_=result[:, a, cols])

        for a in range(5):
            transpose_adj(a)
        for a in range(4):
            group_adj(a)
        for a in range(3):
            quantise_adj(a)
        for pair in range(0, ROW_TILES, 2):
            for a in (pair, pair + 1):
                multiply(a)
            for a in (pair + 5, pair + 6):
                if a < ROW_TILES:
                    transpose_adj(a)
            for a in (pair, pair + 1):
                if a + 4 < ROW_TILES:
                    group_adj(a + 4)
                halves = 2 if a == ROW_TILES - 1 else 1
                width = HIDDEN // halves
                for h in range(halves):
                    finish(a, slice(width * h, width * (h + 1)))
                if a + 3 < ROW_TILES:
                    quantise_adj(a + 3)
